import numpy as np
import ml_dtypes


def mxq(x, axis, fmt="e4m3"):
    dtype, down = {"e4m3": (ml_dtypes.float8_e4m3fn, 7), "e5m2": (ml_dtypes.float8_e5m2, 14)}[fmt]
    v = np.moveaxis(np.asarray(x, np.float32).astype(ml_dtypes.bfloat16).astype(np.float64), axis, -1)
    blocks = v.reshape(v.shape[:-1] + (-1, 32))
    amax = np.abs(blocks).max(-1, keepdims=True)
    byte = np.maximum(np.where(amax > 0, np.frexp(amax)[1] - 1 + 127, 0) - down, 1)
    scale = np.exp2(byte - 127.0)
    codes = (blocks / scale).astype(np.float32).astype(dtype).astype(np.float64)
    return np.moveaxis((codes * scale).reshape(v.shape), -1, axis)


WIDE = False


def mx_kscale(k):
    if not WIDE:
        return np.ones(k)
    levels = np.array([10, -10, 5, -5, 0])
    if k % 512:
        return np.exp2(np.random.permutation(np.resize(levels, k // 32))).repeat(32)
    a = np.empty((k // 512, 16))
    for p in range(k // 512):
        a[p, :8] = np.random.permutation(np.resize(levels, 8))
        for g in range(8):
            far = levels[np.abs(levels - a[p, g]) >= 10]
            a[p, g + 8] = far[np.random.randint(len(far))]
    return np.exp2(a.ravel()).repeat(32)


BF16 = ml_dtypes.bfloat16


def bf(x):
    return np.asarray(x, np.float32).astype(BF16)


def f64(x):
    return np.asarray(x).astype(np.float64)


B, S, E, P, H = 2, 512, 1024, 1024, 8
D = P // H


def rope(x):
    inv_freq = 1.0 / (10000.0 ** (f64(np.arange(0, D, 2)) / D))
    t = f64(np.arange(S))
    freqs = np.repeat(t[:, None] * inv_freq[None, :], 2, axis=-1)
    cos, sin = np.cos(freqs), np.sin(freqs)
    xp = x.reshape(*x.shape[:-1], D // 2, 2)
    rot = np.stack((-xp[..., 1], xp[..., 0]), axis=-1).reshape(x.shape)
    return x * cos + rot * sin


def setup_inputs():
    s = mx_kscale(E)
    return {"emb": bf(np.random.standard_normal((B, S, E)) * s),
            "W1": bf(np.random.standard_normal((P, E)) * 0.6 / np.sqrt(E) / s),
            "W2": bf(np.random.standard_normal((P, E)) * 0.6 / np.sqrt(E) / s),
            "W3": bf(np.random.standard_normal((P, E)) * 2.0 / np.sqrt(E) / s)}


def reference(emb, W1, W2, W3):
    xq = mxq(f64(emb), 2, "e4m3")
    q = (xq @ mxq(f64(W1), 1, "e4m3").T).reshape(B, H, S, D)
    k = (xq @ mxq(f64(W2), 1, "e4m3").T).reshape(B, H, S, D)
    v = (xq @ mxq(f64(W3), 1, "e4m3").T).reshape(B, H, S, D)
    return rope(q), rope(k), v

@@ -1,0 +1,332 @@
+import math
+from contextlib import ExitStack
+
+import concourse.mybir as mybir
+from concourse.masks import make_identity
+
+FLOPS = 2 * 1024 * 1024 * 3072
+
+MANUAL = False
+WQ = {6: 1, 10: 4, 14: 2, 18: 5, 22: 3}
+LEAD = 5
+V0 = 12
+FIN1 = 5
+VADDS = (29, 31)
+LOOK = 2
+FIRST_PAIR = 2
+PAIRED = 28
+FIN1_ACT = True
+
+F32 = mybir.dt.float32
+BF16 = mybir.dt.bfloat16
+I32 = mybir.dt.int32
+U32 = mybir.dt.uint32
+U8 = mybir.dt.uint8
+FP8X4 = mybir.dt.float8_e4m3fn_x4
+ALU = mybir.AluOpType
+ACT = mybir.ActivationFunctionType
+
+P = 128
+
+
+def tile_attention_pa_kernel(tc, emb, W1, W2, W3, out_0, out_1, out_2):
+    nc = tc.nc
+    x2d = emb.flatten_outer_dims()
+    weights = [W1, W2, W3]
+    outs = [o.rearrange("b h (a c) d -> (b h a) (c d)", c=8) for o in (out_0, out_1, out_2)]
+
+    with ExitStack() as ctx:
+        const = ctx.enter_context(tc.tile_pool(name="const", bufs=1))
+        gwp = ctx.enter_context(tc.tile_pool(name="gwp", bufs=2))
+        prodp = ctx.enter_context(tc.tile_pool(name="prodp", bufs=3))
+        yp = ctx.enter_context(tc.tile_pool(name="yp", bufs=6))
+        vp = ctx.enter_context(tc.tile_pool(name="vp", bufs=6))
+        tps = ctx.enter_context(tc.psum_pool(name="tps", bufs=3))
+        accp = ctx.enter_context(tc.psum_pool(name="accp", bufs=3))
+        accvp = ctx.enter_context(tc.psum_pool(name="accvp", bufs=2))
+        if MANUAL:
+            ctx.enter_context(tc.manual_schedule())
+
+        xs = const.tile([P, 8192], BF16, name="xs")
+        ws = [const.tile([P, 4096], BF16, name="ws%d" % g) for g in range(6)]
+        gx = const.tile([P, 8192], BF16, name="gx", align_bytes=64)
+        cx = const.tile([P, 2048], U32, name="cx", align_bytes=64)
+        sx = const.tile([P, 2048], U8, name="sx", align_bytes=64)
+        cw = [const.tile([P, 1024], U32, name="cw%d" % g, align_bytes=64) for g in range(6)]
+        sw = [const.tile([P, 1024], U8, name="sw%d" % g, align_bytes=64) for g in range(6)]
+        ident = const.tile([P, P], F32, name="ident")
+        pos = const.tile([P, 8], F32, name="pos")
+        post = const.tile([P, 8], F32, name="post")
+        freq = const.tile([P, 64], F32, name="freq")
+        warm = const.tile([P, 1], F32, name="warm")
+        turns = [const.tile([P, 256], F32, name="turns%d" % h) for h in range(2)]
+        whole_i = [const.tile([P, 256], I32, name="whole_i%d" % h) for h in range(2)]
+        whole_f = [const.tile([P, 256], F32, name="whole_f%d" % h) for h in range(2)]
+        phase = [const.tile([P, 512], F32, name="phase%d" % h) for h in range(2)]
+        half_sin = [const.tile([P, 512], F32, name="half_sin%d" % h) for h in range(2)]
+        twice_sq = [const.tile([P, 512], F32, name="twice_sq%d" % h) for h in range(2)]
+        tab = const.tile([P, 2048], F32, name="tab")
+
+        xs_w = xs.bitcast(F32)
+        gx_w = gx.bitcast(F32)
+
+        def load_x(j0, j1):
+            nc.sync.dma_start(
+                out=xs[:, 1024 * j0 : 1024 * j1].rearrange("p (j k) -> p j k", k=1024),
+                in_=x2d[P * j0 : P * j1, :].rearrange("(j p) k -> p j k", p=P),
+            )
+
+        def load_w(g, j0, j1):
+            r0 = 512 * (g % 2)
+            nc.sync.dma_start(
+                out=ws[g][:, 1024 * j0 : 1024 * j1].rearrange("p (j k) -> p j k", k=1024),
+                in_=weights[g // 2][r0 + P * j0 : r0 + P * j1, :].rearrange("(j p) k -> p j k", p=P),
+            )
+
+        load_x(0, 1)
+        load_w(0, 0, 2)
+        load_w(0, 2, 4)
+        load_x(1, 2)
+        load_x(2, 4)
+        load_x(4, 6)
+        load_x(6, 8)
+        for g in (1, 4, 2, 5, 3):
+            load_w(g, 0, 4)
+
+        nc.vector.memset(warm, 0.0)
+        nc.scalar.activation(out=warm, in_=warm, func=ACT.Sin)
+        nc.gpsimd.iota(pos[0:64, :], pattern=[[1, 8]], base=0, channel_multiplier=8,
+                       allow_small_or_imprecise_dtypes=True)
+        nc.gpsimd.iota(pos[64:128, :], pattern=[[1, 8]], base=0, channel_multiplier=8,
+                       allow_small_or_imprecise_dtypes=True)
+        make_identity(nc, ident)
+
+        ratio = 10000.0 ** (-1.0 / 64.0)
+        nc.vector.memset(freq[:, 0:1], 1.0)
+        for e in range(6):
+            w = 2 ** e
+            nc.vector.tensor_scalar_mul(out=freq[:, w : 2 * w], in0=freq[:, 0:w], scalar1=ratio ** w)
+        nc.vector.tensor_scalar_mul(out=post, in0=pos, scalar1=1.0 / (2.0 * math.pi))
+
+        tab_p = tab.rearrange("p (s q) -> p s q", s=4)
+        tab_v = tab.rearrange("p (a b q) -> p a q b", a=2, b=2)
+
+        def table_angles(h):
+            nc.vector.tensor_tensor(
+                out=turns[h].rearrange("p (c i) -> p c i", c=4),
+                in0=post[:, 4 * h : 4 * h + 4].unsqueeze(2).to_broadcast([P, 4, 64]),
+                in1=freq.unsqueeze(1).to_broadcast([P, 4, 64]),
+                op=ALU.mult,
+            )
+            nc.vector.tensor_scalar_add(out=whole_i[h], in0=turns[h], scalar1=0.125)
+            nc.vector.tensor_copy(out=whole_f[h], in_=whole_i[h])
+            nc.vector.tensor_tensor(out=phase[h][:, 0:256], in0=turns[h], in1=whole_f[h], op=ALU.subtract)
+            nc.vector.tensor_scalar_add(out=phase[h][:, 256:512], in0=phase[h][:, 0:256], scalar1=-0.25)
+
+        def table_sines(h):
+            nc.scalar.activation(out=half_sin[h], in_=phase[h], func=ACT.Sin, scale=math.pi)
+            nc.scalar.activation(out=twice_sq[h], in_=half_sin[h], func=ACT.Square, scale=math.sqrt(2.0))
+
+        def finish_table(h):
+            q0 = 256 * h
+            nc.vector.tensor_scalar(out=tab_p[:, 0:2, q0 : q0 + 256],
+                                    in0=twice_sq[h].rearrange("p (s q) -> p s q", s=2),
+                                    scalar1=-1.0, scalar2=1.0, op0=ALU.mult, op1=ALU.add)
+            nc.vector.tensor_scalar_add(out=tab_p[:, 2, q0 : q0 + 256], in0=twice_sq[h][:, 256:512], scalar1=-1.0)
+            nc.vector.tensor_scalar(out=tab_p[:, 3, q0 : q0 + 256], in0=twice_sq[h][:, 0:256],
+                                    scalar1=-1.0, scalar2=1.0, op0=ALU.mult, op1=ALU.add)
+
+        def finish_table_act(h):
+            q0 = 256 * h
+            nc.scalar.activation(out=tab_p[:, 0:2, q0 : q0 + 256],
+                                 in_=twice_sq[h].rearrange("p (s q) -> p s q", s=2),
+                                 func=ACT.Copy, scale=-1.0, bias=1.0)
+            nc.scalar.activation(out=tab_p[:, 2, q0 : q0 + 256], in_=twice_sq[h][:, 256:512],
+                                 func=ACT.Copy, scale=1.0, bias=-1.0)
+            nc.scalar.activation(out=tab_p[:, 3, q0 : q0 + 256], in_=twice_sq[h][:, 0:256],
+                                 func=ACT.Copy, scale=-1.0, bias=1.0)
+
+        tbanks = {}
+
+        def transpose_rows(key, src_w, col0):
+            bank = tps.tile([P, 512], F32, name="tbank")
+            for q in range(4):
+                nc.tensor.transpose(out=bank[:, P * q : P * q + P],
+                                    in_=src_w[:, col0 + 256 * (q // 2) + q % 2 : col0 + 256 * (q // 2) + 256 : 2],
+                                    identity=ident)
+            tbanks[key] = bank
+
+        def regroup(eng, dst, key):
+            src = tbanks[key].rearrange("p (g u r) -> p g r u", g=2, u=2)
+            if eng == "s":
+                nc.scalar.copy(out=dst, in_=src)
+            else:
+                nc.vector.tensor_copy(out=dst, in_=src)
+
+        def tx(j):
+            transpose_rows(("x", j), xs_w, 512 * j)
+
+        def cpx(j, eng):
+            regroup(eng, gx_w[:, 512 * j : 512 * j + 512].rearrange("p (g r u) -> p g r u", g=2, u=2), ("x", j))
+
+        def quant_x(j0, j1):
+            nc.vector.quantize_mx(out=cx[:, 256 * j0 : 256 * j1].bitcast(FP8X4),
+                                  scales=sx[:, 256 * j0 : 256 * j1], in_=gx[:, 1024 * j0 : 1024 * j1])
+
+        gws = {}
+
+        def tw(g, j):
+            transpose_rows((g, j), ws[g].bitcast(F32), 512 * j)
+
+        def cpw(g, j, eng):
+            if g not in gws:
+                gws[g] = gwp.tile([P, 4096], BF16, name="gw", align_bytes=64)
+            dst4 = gws[g].bitcast(F32).rearrange("p (g n u) -> p g n u", g=2, u=2)
+            regroup(eng, dst4[:, :, P * j : P * j + P, :], (g, j))
+
+        def quant_w(g, pieces):
+            n = 4096 // pieces
+            for i in range(pieces):
+                nc.vector.quantize_mx(out=cw[g][:, (n // 4) * i : (n // 4) * (i + 1)].bitcast(FP8X4),
+                                      scales=sw[g][:, (n // 4) * i : (n // 4) * (i + 1)],
+                                      in_=gws[g][:, n * i : n * (i + 1)])
+
+        def quant_w0(f):
+            for h in range(2):
+                c0 = 512 * h + 256 * f
+                nc.vector.quantize_mx(out=cw[0][:, c0 : c0 + 256].bitcast(FP8X4), scales=sw[0][:, c0 : c0 + 256],
+                                      in_=gws[0][:, 4 * c0 : 4 * c0 + 1024])
+
+        def project0(acc, f):
+            for h in range(2):
+                c0 = 512 * h + 256 * f
+                nc.tensor.matmul_mx(out=acc,
+                                    lhsT=cx[:, P * h : P * h + P].bitcast(FP8X4), lhsT_scale=sx[:, P * h : P * h + P],
+                                    rhs=cw[0][:, c0 : c0 + 256].bitcast(FP8X4), rhs_scale=sw[0][:, c0 : c0 + 256],
+                                    start=(h == 0), stop=(h == 1))
+
+        def project(pool, m, g):
+            acc = pool.tile([P, 512], F32, name="acc")
+            for h in range(2):
+                c0 = 256 * m + P * h
+                nc.tensor.matmul_mx(out=acc,
+                                    lhsT=cx[:, c0 : c0 + P].bitcast(FP8X4), lhsT_scale=sx[:, c0 : c0 + P],
+                                    rhs=cw[g][:, 512 * h : 512 * h + 512].bitcast(FP8X4),
+                                    rhs_scale=sw[g][:, 512 * h : 512 * h + 512],
+                                    start=(h == 0), stop=(h == 1))
+            return acc
+
+        pair = {}
+
+        def rotate(k, m, g, acc):
+            half = g % 2
+            if FIRST_PAIR <= k < PAIRED:
+                if k % 2 == 0:
+                    pair["prod"] = prodp.tile([P, 2048], F32, name="prod2")
+                prod = pair["prod"][:, 1024 * (k % 2) : 1024 * (k % 2) + 1024]
+            else:
+                prod = prodp.tile([P, 1024], F32, name="prod", tag="prod2")
+            pieces = 2 if k == 0 else 1
+            n = 256 // pieces
+            for f in range(pieces):
+                nc.vector.tensor_tensor(
+                    out=prod.rearrange("p (a q b) -> p a q b", a=2, b=2)[:, :, n * f : n * f + n, :],
+                    in0=(acc[f] if k == 0 else acc).rearrange("p (q a) -> p a q", a=2).unsqueeze(3).to_broadcast([P, 2, n, 2]),
+                    in1=tab_v[:, :, 256 * half + n * f : 256 * half + n * f + n, :],
+                    op=ALU.mult,
+                )
+            if FIRST_PAIR <= k < PAIRED:
+                if k % 2 == 1:
+                    both = pair["prod"].rearrange("p (j a n) -> p j a n", j=2, a=2)
+                    y2 = yp.tile([P, 2, 512], F32, name="y2")
+                    nc.gpsimd.tensor_tensor(out=y2, in0=both[:, :, 0, :], in1=both[:, :, 1, :], op=ALU.add)
+                    nc.sync.dma_start(
+                        out=outs[g // 2][P * (m - 1) : P * (m + 1), 512 * half : 512 * half + 512].rearrange(
+                            "(j p) n -> p j n", p=P),
+                        in_=y2)
+                return
+            y = yp.tile([P, 512], F32, name="y", tag="y2")
+            if k in VADDS:
+                nc.vector.tensor_tensor(out=y, in0=prod[:, 0:512], in1=prod[:, 512:1024], op=ALU.add)
+            else:
+                nc.gpsimd.tensor_tensor(out=y, in0=prod[:, 0:512], in1=prod[:, 512:1024], op=ALU.add)
+            nc.sync.dma_start(out=outs[g // 2][P * m : P * m + P, 512 * half : 512 * half + 512], in_=y)
+
+        vaccs = {}
+
+        def value_mm(i):
+            vaccs[i] = project(accvp, i % 8, 4 + i // 8)
+
+        def value_out(i):
+            m = i % 8
+            half = i // 8
+            v = vp.tile([P, 512], F32, name="v")
+            nc.scalar.copy(out=v, in_=vaccs[i])
+            nc.sync.dma_start(out=outs[2][P * m : P * m + P, 512 * half : 512 * half + 512], in_=v)
+
+        banks = [(m, g) for g in range(4) for m in range(8)]
+        accs = {}
+
+        table_angles(0)
+        table_sines(0)
+        table_angles(1)
+        tx(0)
+        cpx(0, "v")
+        tw(0, 0)
+        tw(0, 1)
+        cpw(0, 0, "s")
+        cpw(0, 1, "v")
+        quant_x(0, 1)
+        finish_table(0)
+        quant_w0(0)
+        acc0 = [accp.tile([P, 256], F32, name="acc") for f in range(2)]
+        accs[0] = acc0
+        tw(0, 2)
+        tw(0, 3)
+        project0(acc0[0], 0)
+        cpw(0, 2, "s")
+        cpw(0, 3, "v")
+        quant_w0(1)
+        tx(1)
+        project0(acc0[1], 1)
+        cpx(1, "s")
+        tx(2)
+        tx(3)
+        cpx(2, "s")
+        cpx(3, "s")
+        quant_x(1, 2)
+        tx(4)
+        tx(5)
+        accs[1] = project(accp, 1, 0)
+        cpx(4, "s")
+        cpx(5, "s")
+        quant_x(2, 4)
+        tx(6)
+        tx(7)
+        cpx(6, "s")
+        cpx(7, "s")
+
+        for k in range(32):
+            if k == 1:
+                quant_x(4, 8)
+            if k == FIN1 and not FIN1_ACT:
+                finish_table(1)
+            if k in WQ:
+                quant_w(WQ[k], 1)
+            if k + LOOK < 32:
+                accs[k + LOOK] = project(accp, banks[k + LOOK][0], banks[k + LOOK][1])
+            if k >= V0 and k - V0 < 16:
+                value_mm(k - V0)
+            if k == 2:
+                table_sines(1)
+                if FIN1_ACT:
+                    finish_table_act(1)
+            for d, js in ((LEAD, (0, 1)), (LEAD - 1, (2, 3))):
+                if k + d in WQ:
+                    for j in js:
+                        tw(WQ[k + d], j)
+                    for j in js:
+                        cpw(WQ[k + d], j, "s")
+            if k >= V0 and k - V0 < 16:
+                value_out(k - V0)
+            rotate(k, banks[k][0], banks[k][1], accs[k])

@@ -6,16 +6,14 @@ from concourse.masks import make_identity
 
 FLOPS = 2 * 1024 * 1024 * 3072
 
-MANUAL = False
-WQ = {6: 1, 10: 4, 14: 2, 18: 5, 22: 3}
-LEAD = 5
+WQ = {5: 1, 9: 4, 13: 2, 17: 5, 21: 3}
+TW = {2: (1, (0, 1)), 3: (1, (2, 3)), 5: (4, (0, 1)), 6: (4, (2, 3)), 8: (2, (0, 1)), 9: (2, (2, 3)),
+      12: (5, (0, 1)), 13: (5, (2, 3)), 16: (3, (0, 1)), 17: (3, (2, 3))}
 V0 = 12
-FIN1 = 5
 VADDS = (29, 31)
 LOOK = 2
 FIRST_PAIR = 2
 PAIRED = 28
-FIN1_ACT = True
 
 F32 = mybir.dt.float32
 BF16 = mybir.dt.bfloat16
@@ -44,8 +42,6 @@ def tile_attention_pa_kernel(tc, emb, W1, W2, W3, out_0, out_1, out_2):
         tps = ctx.enter_context(tc.psum_pool(name="tps", bufs=3))
         accp = ctx.enter_context(tc.psum_pool(name="accp", bufs=3))
         accvp = ctx.enter_context(tc.psum_pool(name="accvp", bufs=2))
-        if MANUAL:
-            ctx.enter_context(tc.manual_schedule())
 
         xs = const.tile([P, 8192], BF16, name="xs")
         ws = [const.tile([P, 4096], BF16, name="ws%d" % g) for g in range(6)]
@@ -58,13 +54,12 @@ def tile_attention_pa_kernel(tc, emb, W1, W2, W3, out_0, out_1, out_2):
         pos = const.tile([P, 8], F32, name="pos")
         post = const.tile([P, 8], F32, name="post")
         freq = const.tile([P, 64], F32, name="freq")
+        half_pi = const.tile([P, 1], F32, name="half_pi")
         warm = const.tile([P, 1], F32, name="warm")
         turns = [const.tile([P, 256], F32, name="turns%d" % h) for h in range(2)]
-        whole_i = [const.tile([P, 256], I32, name="whole_i%d" % h) for h in range(2)]
-        whole_f = [const.tile([P, 256], F32, name="whole_f%d" % h) for h in range(2)]
-        phase = [const.tile([P, 512], F32, name="phase%d" % h) for h in range(2)]
-        half_sin = [const.tile([P, 512], F32, name="half_sin%d" % h) for h in range(2)]
-        twice_sq = [const.tile([P, 512], F32, name="twice_sq%d" % h) for h in range(2)]
+        whole = [const.tile([P, 256], I32, name="whole%d" % h) for h in range(2)]
+        phase = [const.tile([P, 256], F32, name="phase%d" % h) for h in range(2)]
+        fold = [const.tile([P, 256], F32, name="fold%d" % h) for h in range(2)]
         tab = const.tile([P, 2048], F32, name="tab")
 
         xs_w = xs.bitcast(F32)
@@ -76,24 +71,25 @@ def tile_attention_pa_kernel(tc, emb, W1, W2, W3, out_0, out_1, out_2):
                 in_=x2d[P * j0 : P * j1, :].rearrange("(j p) k -> p j k", p=P),
             )
 
-        def load_w(g, j0, j1):
+        def load_w(g, b0, b1):
             r0 = 512 * (g % 2)
             nc.sync.dma_start(
-                out=ws[g][:, 1024 * j0 : 1024 * j1].rearrange("p (j k) -> p j k", k=1024),
-                in_=weights[g // 2][r0 + P * j0 : r0 + P * j1, :].rearrange("(j p) k -> p j k", p=P),
+                out=ws[g][:, 2048 * b0 : 2048 * b1].rearrange("p (b j) -> p b j", j=2048),
+                in_=weights[g // 2][r0 + 256 * b0 : r0 + 256 * b1, :].rearrange("(b p j) k -> p b (j k)", p=P, j=2),
             )
 
         load_x(0, 1)
-        load_w(0, 0, 2)
-        load_w(0, 2, 4)
+        load_w(0, 0, 1)
+        load_w(0, 1, 2)
         load_x(1, 2)
         load_x(2, 4)
         load_x(4, 6)
         load_x(6, 8)
         for g in (1, 4, 2, 5, 3):
-            load_w(g, 0, 4)
+            load_w(g, 0, 2)
 
-        nc.vector.memset(warm, 0.0)
+        nc.gpsimd.memset(warm, 0.0)
+        nc.gpsimd.tensor_scalar(out=half_pi, in0=warm, scalar1=1.0, scalar2=0.5 * math.pi, op0=ALU.mult, op1=ALU.add)
         nc.scalar.activation(out=warm, in_=warm, func=ACT.Sin)
         nc.gpsimd.iota(pos[0:64, :], pattern=[[1, 8]], base=0, channel_multiplier=8,
                        allow_small_or_imprecise_dtypes=True)
@@ -108,52 +104,42 @@ def tile_attention_pa_kernel(tc, emb, W1, W2, W3, out_0, out_1, out_2):
             nc.vector.tensor_scalar_mul(out=freq[:, w : 2 * w], in0=freq[:, 0:w], scalar1=ratio ** w)
         nc.vector.tensor_scalar_mul(out=post, in0=pos, scalar1=1.0 / (2.0 * math.pi))
 
-        tab_p = tab.rearrange("p (s q) -> p s q", s=4)
-        tab_v = tab.rearrange("p (a b q) -> p a q b", a=2, b=2)
+        tab_s = tab.rearrange("p (h b q r) -> p h q b r", h=2, b=2, q=4)
+        tab_v = tab.rearrange("p (h c s r) -> p h c r s", h=2, c=4, s=2)
 
-        def table_angles(h):
-            nc.vector.tensor_tensor(
-                out=turns[h].rearrange("p (c i) -> p c i", c=4),
-                in0=post[:, 4 * h : 4 * h + 4].unsqueeze(2).to_broadcast([P, 4, 64]),
-                in1=freq.unsqueeze(1).to_broadcast([P, 4, 64]),
-                op=ALU.mult,
+        def table_turns(h):
+            angle_args = (
+                post[:, 4 * h : 4 * h + 4].unsqueeze(2).to_broadcast([P, 4, 64]),
+                freq.unsqueeze(1).to_broadcast([P, 4, 64]),
             )
-            nc.vector.tensor_scalar_add(out=whole_i[h], in0=turns[h], scalar1=0.125)
-            nc.vector.tensor_copy(out=whole_f[h], in_=whole_i[h])
-            nc.vector.tensor_tensor(out=phase[h][:, 0:256], in0=turns[h], in1=whole_f[h], op=ALU.subtract)
-            nc.vector.tensor_scalar_add(out=phase[h][:, 256:512], in0=phase[h][:, 0:256], scalar1=-0.25)
+            nc.vector.scalar_tensor_tensor(out=whole[h].rearrange("p (c i) -> p c i", c=4), in0=angle_args[0],
+                                           scalar=1.0, in1=angle_args[1], op0=ALU.mult, op1=ALU.mult)
+            nc.vector.tensor_tensor(out=turns[h].rearrange("p (c i) -> p c i", c=4), in0=angle_args[0],
+                                    in1=angle_args[1], op=ALU.mult)
+
+        def table_phase(h):
+            nc.vector.tensor_tensor(out=phase[h], in0=turns[h], in1=whole[h], op=ALU.subtract)
+
+        def by_block(t):
+            return t.rearrange("p (b r) -> p b r", b=2)
 
         def table_sines(h):
-            nc.scalar.activation(out=half_sin[h], in_=phase[h], func=ACT.Sin, scale=math.pi)
-            nc.scalar.activation(out=twice_sq[h], in_=half_sin[h], func=ACT.Square, scale=math.sqrt(2.0))
+            ph, fo = by_block(phase[h]), by_block(fold[h])
+            nc.scalar.activation(out=tab_s[:, h, 1], in_=ph, func=ACT.Sin, scale=2.0 * math.pi)
+            nc.scalar.activation(out=fo, in_=ph, func=ACT.Abs)
+            nc.scalar.activation(out=tab_s[:, h, 0], in_=fo, func=ACT.Sin, scale=-2.0 * math.pi, bias=half_pi)
 
-        def finish_table(h):
-            q0 = 256 * h
-            nc.vector.tensor_scalar(out=tab_p[:, 0:2, q0 : q0 + 256],
-                                    in0=twice_sq[h].rearrange("p (s q) -> p s q", s=2),
-                                    scalar1=-1.0, scalar2=1.0, op0=ALU.mult, op1=ALU.add)
-            nc.vector.tensor_scalar_add(out=tab_p[:, 2, q0 : q0 + 256], in0=twice_sq[h][:, 256:512], scalar1=-1.0)
-            nc.vector.tensor_scalar(out=tab_p[:, 3, q0 : q0 + 256], in0=twice_sq[h][:, 0:256],
-                                    scalar1=-1.0, scalar2=1.0, op0=ALU.mult, op1=ALU.add)
-
-        def finish_table_act(h):
-            q0 = 256 * h
-            nc.scalar.activation(out=tab_p[:, 0:2, q0 : q0 + 256],
-                                 in_=twice_sq[h].rearrange("p (s q) -> p s q", s=2),
-                                 func=ACT.Copy, scale=-1.0, bias=1.0)
-            nc.scalar.activation(out=tab_p[:, 2, q0 : q0 + 256], in_=twice_sq[h][:, 256:512],
-                                 func=ACT.Copy, scale=1.0, bias=-1.0)
-            nc.scalar.activation(out=tab_p[:, 3, q0 : q0 + 256], in_=twice_sq[h][:, 0:256],
-                                 func=ACT.Copy, scale=-1.0, bias=1.0)
+        def table_copies(h):
+            nc.vector.tensor_scalar_mul(out=tab_s[:, h, 2], in0=tab_s[:, h, 1], scalar1=-1.0)
+            nc.vector.tensor_copy(out=tab_s[:, h, 3], in_=tab_s[:, h, 0])
 
         tbanks = {}
 
         def transpose_rows(key, src_w, col0):
             bank = tps.tile([P, 512], F32, name="tbank")
             for q in range(4):
-                nc.tensor.transpose(out=bank[:, P * q : P * q + P],
-                                    in_=src_w[:, col0 + 256 * (q // 2) + q % 2 : col0 + 256 * (q // 2) + 256 : 2],
-                                    identity=ident)
+                c0 = col0 + 256 * (q // 2)
+                nc.tensor.transpose(out=bank[:, P * q : P * q + P], in_=src_w[:, c0 + q % 2 : c0 + 256 : 2], identity=ident)
             tbanks[key] = bank
 
         def regroup(eng, dst, key):
@@ -184,12 +170,8 @@ def tile_attention_pa_kernel(tc, emb, W1, W2, W3, out_0, out_1, out_2):
             dst4 = gws[g].bitcast(F32).rearrange("p (g n u) -> p g n u", g=2, u=2)
             regroup(eng, dst4[:, :, P * j : P * j + P, :], (g, j))
 
-        def quant_w(g, pieces):
-            n = 4096 // pieces
-            for i in range(pieces):
-                nc.vector.quantize_mx(out=cw[g][:, (n // 4) * i : (n // 4) * (i + 1)].bitcast(FP8X4),
-                                      scales=sw[g][:, (n // 4) * i : (n // 4) * (i + 1)],
-                                      in_=gws[g][:, n * i : n * (i + 1)])
+        def quant_w(g):
+            nc.vector.quantize_mx(out=cw[g].bitcast(FP8X4), scales=sw[g], in_=gws[g])
 
         def quant_w0(f):
             for h in range(2):
@@ -218,38 +200,42 @@ def tile_attention_pa_kernel(tc, emb, W1, W2, W3, out_0, out_1, out_2):
 
         pair = {}
 
+        def multiply(prod, acc, half, c0, c1):
+            nc.vector.tensor_tensor(
+                out=prod.rearrange("p (c r s) -> p c r s", c=4, s=2)[:, c0:c1],
+                in0=acc.rearrange("p (c r) -> p c r", r=P).unsqueeze(3).to_broadcast([P, c1 - c0, P, 2]),
+                in1=tab_v[:, half, c0:c1],
+                op=ALU.mult,
+            )
+
+        prod0 = prodp.tile([P, 1024], F32, name="prod", tag="prod2")
+
         def rotate(k, m, g, acc):
             half = g % 2
-            if FIRST_PAIR <= k < PAIRED:
+            if k == 0:
+                prod = prod0
+            elif FIRST_PAIR <= k < PAIRED:
                 if k % 2 == 0:
                     pair["prod"] = prodp.tile([P, 2048], F32, name="prod2")
                 prod = pair["prod"][:, 1024 * (k % 2) : 1024 * (k % 2) + 1024]
             else:
                 prod = prodp.tile([P, 1024], F32, name="prod", tag="prod2")
-            pieces = 2 if k == 0 else 1
-            n = 256 // pieces
-            for f in range(pieces):
-                nc.vector.tensor_tensor(
-                    out=prod.rearrange("p (a q b) -> p a q b", a=2, b=2)[:, :, n * f : n * f + n, :],
-                    in0=(acc[f] if k == 0 else acc).rearrange("p (q a) -> p a q", a=2).unsqueeze(3).to_broadcast([P, 2, n, 2]),
-                    in1=tab_v[:, :, 256 * half + n * f : 256 * half + n * f + n, :],
-                    op=ALU.mult,
-                )
+            if k:
+                multiply(prod, acc, half, 0, 4)
             if FIRST_PAIR <= k < PAIRED:
                 if k % 2 == 1:
-                    both = pair["prod"].rearrange("p (j a n) -> p j a n", j=2, a=2)
-                    y2 = yp.tile([P, 2, 512], F32, name="y2")
-                    nc.gpsimd.tensor_tensor(out=y2, in0=both[:, :, 0, :], in1=both[:, :, 1, :], op=ALU.add)
+                    both = pair["prod"].rearrange("p (j a n) -> p j a n", a=2, n=256)
+                    y2 = yp.tile([P, 1024], F32, name="y2")
+                    nc.gpsimd.tensor_tensor(out=y2.rearrange("p (j n) -> p j n", n=256), in0=both[:, :, 0], in1=both[:, :, 1], op=ALU.add)
                     nc.sync.dma_start(
                         out=outs[g // 2][P * (m - 1) : P * (m + 1), 512 * half : 512 * half + 512].rearrange(
                             "(j p) n -> p j n", p=P),
-                        in_=y2)
+                        in_=y2.rearrange("p (j n) -> p j n", n=512))
                 return
             y = yp.tile([P, 512], F32, name="y", tag="y2")
-            if k in VADDS:
-                nc.vector.tensor_tensor(out=y, in0=prod[:, 0:512], in1=prod[:, 512:1024], op=ALU.add)
-            else:
-                nc.gpsimd.tensor_tensor(out=y, in0=prod[:, 0:512], in1=prod[:, 512:1024], op=ALU.add)
+            both = prod.rearrange("p (j a n) -> p j a n", a=2, n=256)
+            eng = nc.vector if k in VADDS else nc.gpsimd
+            eng.tensor_tensor(out=y.rearrange("p (j n) -> p j n", n=256), in0=both[:, :, 0], in1=both[:, :, 1], op=ALU.add)
             nc.sync.dma_start(out=outs[g // 2][P * m : P * m + P, 512 * half : 512 * half + 512], in_=y)
 
         vaccs = {}
@@ -261,72 +247,74 @@ def tile_attention_pa_kernel(tc, emb, W1, W2, W3, out_0, out_1, out_2):
             m = i % 8
             half = i // 8
             v = vp.tile([P, 512], F32, name="v")
-            nc.scalar.copy(out=v, in_=vaccs[i])
+            nc.scalar.copy(out=v.rearrange("p (b r j) -> p b r j", b=2, j=2),
+                           in_=vaccs[i].rearrange("p (b j r) -> p b r j", b=2, j=2))
             nc.sync.dma_start(out=outs[2][P * m : P * m + P, 512 * half : 512 * half + 512], in_=v)
 
         banks = [(m, g) for g in range(4) for m in range(8)]
         accs = {}
 
-        table_angles(0)
-        table_sines(0)
-        table_angles(1)
+        ctx.enter_context(tc.manual_schedule(engines={mybir.EngineType.PE, mybir.EngineType.Activation,
+                                                      mybir.EngineType.DVE, mybir.EngineType.Pool}))
+        table_turns(0)
+        table_phase(0)
         tx(0)
         cpx(0, "v")
+        table_sines(0)
+        quant_x(0, 1)
+        table_turns(1)
         tw(0, 0)
         tw(0, 1)
         cpw(0, 0, "s")
+        table_copies(0)
         cpw(0, 1, "v")
-        quant_x(0, 1)
-        finish_table(0)
         quant_w0(0)
-        acc0 = [accp.tile([P, 256], F32, name="acc") for f in range(2)]
-        accs[0] = acc0
         tw(0, 2)
         tw(0, 3)
-        project0(acc0[0], 0)
         cpw(0, 2, "s")
         cpw(0, 3, "v")
-        quant_w0(1)
         tx(1)
-        project0(acc0[1], 1)
         cpx(1, "s")
+        acc0 = [accp.tile([P, 256], F32, name="acc") for f in range(2)]
+        accs[0] = acc0
+        project0(acc0[0], 0)
+        multiply(prod0, acc0[0], 0, 0, 2)
+        quant_w0(1)
+        quant_x(1, 2)
         tx(2)
         tx(3)
         cpx(2, "s")
         cpx(3, "s")
-        quant_x(1, 2)
-        tx(4)
-        tx(5)
+        project0(acc0[1], 1)
         accs[1] = project(accp, 1, 0)
-        cpx(4, "s")
-        cpx(5, "s")
+        multiply(prod0, acc0[1], 0, 2, 4)
         quant_x(2, 4)
-        tx(6)
-        tx(7)
-        cpx(6, "s")
-        cpx(7, "s")
 
         for k in range(32):
-            if k == 1:
-                quant_x(4, 8)
-            if k == FIN1 and not FIN1_ACT:
-                finish_table(1)
+            if k < 2:
+                for j in (4 + 2 * k, 5 + 2 * k):
+                    tx(j)
+                for j in (4 + 2 * k, 5 + 2 * k):
+                    cpx(j, "s")
+            if k in TW:
+                g, js = TW[k]
+                for j in js:
+                    tw(g, j)
+                for j in js:
+                    cpw(g, j, "s")
+            rotate(k, banks[k][0], banks[k][1], accs[k])
+            if k == 2:
+                quant_x(4, 6)
+                table_phase(1)
+            if k == 3:
+                quant_x(6, 8)
+                table_sines(1)
+            if k == 4:
+                table_copies(1)
             if k in WQ:
-                quant_w(WQ[k], 1)
+                quant_w(WQ[k])
             if k + LOOK < 32:
                 accs[k + LOOK] = project(accp, banks[k + LOOK][0], banks[k + LOOK][1])
             if k >= V0 and k - V0 < 16:
                 value_mm(k - V0)
-            if k == 2:
-                table_sines(1)
-                if FIN1_ACT:
-                    finish_table_act(1)
-            for d, js in ((LEAD, (0, 1)), (LEAD - 1, (2, 3))):
-                if k + d in WQ:
-                    for j in js:
-                        tw(WQ[k + d], j)
-                    for j in js:
-                        cpw(WQ[k + d], j, "s")
-            if k >= V0 and k - V0 < 16:
                 value_out(k - V0)
-            rotate(k, banks[k][0], banks[k][1], accs[k])

@@ -45,6 +45,7 @@ def tile_attention_pa_kernel(tc, emb, W1, W2, W3, out_0, out_1, out_2):
 
         xs = const.tile([P, 8192], BF16, name="xs")
         ws = [const.tile([P, 4096], BF16, name="ws%d" % g) for g in range(6)]
+        gw0 = [const.tile([P, 1024], BF16, name="gw0_%d" % j, align_bytes=64) for j in range(4)]
         gx = const.tile([P, 8192], BF16, name="gx", align_bytes=64)
         cx = const.tile([P, 2048], U32, name="cx", align_bytes=64)
         sx = const.tile([P, 2048], U8, name="sx", align_bytes=64)
@@ -107,15 +108,20 @@ def tile_attention_pa_kernel(tc, emb, W1, W2, W3, out_0, out_1, out_2):
         tab_s = tab.rearrange("p (h b q r) -> p h q b r", h=2, b=2, q=4)
         tab_v = tab.rearrange("p (h c s r) -> p h c r s", h=2, c=4, s=2)
 
-        def table_turns(h):
-            angle_args = (
-                post[:, 4 * h : 4 * h + 4].unsqueeze(2).to_broadcast([P, 4, 64]),
-                freq.unsqueeze(1).to_broadcast([P, 4, 64]),
-            )
-            nc.vector.scalar_tensor_tensor(out=whole[h].rearrange("p (c i) -> p c i", c=4), in0=angle_args[0],
-                                           scalar=1.0, in1=angle_args[1], op0=ALU.mult, op1=ALU.mult)
-            nc.vector.tensor_tensor(out=turns[h].rearrange("p (c i) -> p c i", c=4), in0=angle_args[0],
-                                    in1=angle_args[1], op=ALU.mult)
+        def angle_args(h):
+            return (post[:, 4 * h : 4 * h + 4].unsqueeze(2).to_broadcast([P, 4, 64]),
+                    freq.unsqueeze(1).to_broadcast([P, 4, 64]))
+
+        def table_turns_v(h):
+            in0, in1 = angle_args(h)
+            nc.vector.tensor_tensor(out=turns[h].rearrange("p (c i) -> p c i", c=4), in0=in0, in1=in1, op=ALU.mult)
+            nc.vector.scalar_tensor_tensor(out=whole[h].rearrange("p (c i) -> p c i", c=4), in0=in0,
+                                           scalar=1.0, in1=in1, op0=ALU.mult, op1=ALU.mult)
+
+        def table_turns_g(h):
+            in0, in1 = angle_args(h)
+            nc.gpsimd.tensor_tensor(out=turns[h].rearrange("p (c i) -> p c i", c=4), in0=in0, in1=in1, op=ALU.mult)
+            nc.gpsimd.tensor_scalar(out=whole[h], in0=turns[h], scalar1=1.0, scalar2=0.0, op0=ALU.mult, op1=ALU.add)
 
         def table_phase(h):
             nc.vector.tensor_tensor(out=phase[h], in0=turns[h], in1=whole[h], op=ALU.subtract)
@@ -123,14 +129,19 @@ def tile_attention_pa_kernel(tc, emb, W1, W2, W3, out_0, out_1, out_2):
         def by_block(t):
             return t.rearrange("p (b r) -> p b r", b=2)
 
-        def table_sines(h):
-            ph, fo = by_block(phase[h]), by_block(fold[h])
-            nc.scalar.activation(out=tab_s[:, h, 1], in_=ph, func=ACT.Sin, scale=2.0 * math.pi)
-            nc.scalar.activation(out=fo, in_=ph, func=ACT.Abs)
-            nc.scalar.activation(out=tab_s[:, h, 0], in_=fo, func=ACT.Sin, scale=-2.0 * math.pi, bias=half_pi)
+        def sine(h):
+            nc.scalar.activation(out=tab_s[:, h, 1], in_=by_block(phase[h]), func=ACT.Sin, scale=2.0 * math.pi)
 
-        def table_copies(h):
+        def fold_phase(h):
+            nc.scalar.activation(out=fold[h], in_=phase[h], func=ACT.Abs)
+
+        def cosine(h):
+            nc.scalar.activation(out=tab_s[:, h, 0], in_=by_block(fold[h]), func=ACT.Sin, scale=-2.0 * math.pi, bias=half_pi)
+
+        def copy_sine(h):
             nc.vector.tensor_scalar_mul(out=tab_s[:, h, 2], in0=tab_s[:, h, 1], scalar1=-1.0)
+
+        def copy_cosine(h):
             nc.vector.tensor_copy(out=tab_s[:, h, 3], in_=tab_s[:, h, 0])
 
         tbanks = {}
@@ -165,6 +176,9 @@ def tile_attention_pa_kernel(tc, emb, W1, W2, W3, out_0, out_1, out_2):
             transpose_rows((g, j), ws[g].bitcast(F32), 512 * j)
 
         def cpw(g, j, eng):
+            if g == 0:
+                regroup(eng, gw0[j].bitcast(F32).rearrange("p (g n u) -> p g n u", g=2, u=2), (g, j))
+                return
             if g not in gws:
                 gws[g] = gwp.tile([P, 4096], BF16, name="gw", align_bytes=64)
             dst4 = gws[g].bitcast(F32).rearrange("p (g n u) -> p g n u", g=2, u=2)
@@ -173,11 +187,11 @@ def tile_attention_pa_kernel(tc, emb, W1, W2, W3, out_0, out_1, out_2):
         def quant_w(g):
             nc.vector.quantize_mx(out=cw[g].bitcast(FP8X4), scales=sw[g], in_=gws[g])
 
-        def quant_w0(f):
+        def quant_w0(j):
             for h in range(2):
-                c0 = 512 * h + 256 * f
-                nc.vector.quantize_mx(out=cw[0][:, c0 : c0 + 256].bitcast(FP8X4), scales=sw[0][:, c0 : c0 + 256],
-                                      in_=gws[0][:, 4 * c0 : 4 * c0 + 1024])
+                c0 = 512 * h + P * j
+                nc.vector.quantize_mx(out=cw[0][:, c0 : c0 + P].bitcast(FP8X4), scales=sw[0][:, c0 : c0 + P],
+                                      in_=gw0[j][:, 512 * h : 512 * h + 512])
 
         def project0(acc, f):
             for h in range(2):
@@ -256,30 +270,35 @@ def tile_attention_pa_kernel(tc, emb, W1, W2, W3, out_0, out_1, out_2):
 
         ctx.enter_context(tc.manual_schedule(engines={mybir.EngineType.PE, mybir.EngineType.Activation,
                                                       mybir.EngineType.DVE, mybir.EngineType.Pool}))
-        table_turns(0)
+        table_turns_v(0)
+        table_turns_g(1)
         table_phase(0)
         tx(0)
         cpx(0, "v")
-        table_sines(0)
+        sine(0)
+        fold_phase(0)
         quant_x(0, 1)
-        table_turns(1)
         tw(0, 0)
         tw(0, 1)
         cpw(0, 0, "s")
-        table_copies(0)
+        cosine(0)
+        copy_sine(0)
         cpw(0, 1, "v")
         quant_w0(0)
+        quant_w0(1)
         tw(0, 2)
         tw(0, 3)
         cpw(0, 2, "s")
         cpw(0, 3, "v")
+        copy_cosine(0)
         tx(1)
         cpx(1, "s")
         acc0 = [accp.tile([P, 256], F32, name="acc") for f in range(2)]
         accs[0] = acc0
         project0(acc0[0], 0)
         multiply(prod0, acc0[0], 0, 0, 2)
-        quant_w0(1)
+        quant_w0(2)
+        quant_w0(3)
         quant_x(1, 2)
         tx(2)
         tx(3)
@@ -308,9 +327,12 @@ def tile_attention_pa_kernel(tc, emb, W1, W2, W3, out_0, out_1, out_2):
                 table_phase(1)
             if k == 3:
                 quant_x(6, 8)
-                table_sines(1)
-            if k == 4:
-                table_copies(1)
+                sine(1)
+                fold_phase(1)
+                cosine(1)
+            if k == 6:
+                copy_sine(1)
+                copy_cosine(1)
             if k in WQ:
                 quant_w(WQ[k])
             if k + LOOK < 32:

@@ -9,7 +9,7 @@ FLOPS = 2 * 1024 * 1024 * 3072
 WQ = {5: 1, 9: 4, 13: 2, 17: 5, 21: 3}
 TW = {2: (1, (0, 1)), 3: (1, (2, 3)), 5: (4, (0, 1)), 6: (4, (2, 3)), 8: (2, (0, 1)), 9: (2, (2, 3)),
       12: (5, (0, 1)), 13: (5, (2, 3)), 16: (3, (0, 1)), 17: (3, (2, 3))}
-V0 = 12
+V0 = 11
 VADDS = (29, 31)
 LOOK = 2
 FIRST_PAIR = 2
@@ -36,7 +36,7 @@ def tile_attention_pa_kernel(tc, emb, W1, W2, W3, out_0, out_1, out_2):
     with ExitStack() as ctx:
         const = ctx.enter_context(tc.tile_pool(name="const", bufs=1))
         gwp = ctx.enter_context(tc.tile_pool(name="gwp", bufs=2))
-        prodp = ctx.enter_context(tc.tile_pool(name="prodp", bufs=3))
+        prodp = ctx.enter_context(tc.tile_pool(name="prodp", bufs=5))
         yp = ctx.enter_context(tc.tile_pool(name="yp", bufs=6))
         vp = ctx.enter_context(tc.tile_pool(name="vp", bufs=6))
         tps = ctx.enter_context(tc.psum_pool(name="tps", bufs=3))
@@ -129,14 +129,14 @@ def tile_attention_pa_kernel(tc, emb, W1, W2, W3, out_0, out_1, out_2):
         def by_block(t):
             return t.rearrange("p (b r) -> p b r", b=2)
 
-        def sine(h):
-            nc.scalar.activation(out=tab_s[:, h, 1], in_=by_block(phase[h]), func=ACT.Sin, scale=2.0 * math.pi)
+        def sine(h, q, sign):
+            nc.scalar.activation(out=tab_s[:, h, q], in_=by_block(phase[h]), func=ACT.Sin, scale=sign * 2.0 * math.pi)
 
         def fold_phase(h):
             nc.scalar.activation(out=fold[h], in_=phase[h], func=ACT.Abs)
 
-        def cosine(h):
-            nc.scalar.activation(out=tab_s[:, h, 0], in_=by_block(fold[h]), func=ACT.Sin, scale=-2.0 * math.pi, bias=half_pi)
+        def cosine(h, q):
+            nc.scalar.activation(out=tab_s[:, h, q], in_=by_block(fold[h]), func=ACT.Sin, scale=-2.0 * math.pi, bias=half_pi)
 
         def copy_sine(h):
             nc.vector.tensor_scalar_mul(out=tab_s[:, h, 2], in0=tab_s[:, h, 1], scalar1=-1.0)
@@ -227,30 +227,30 @@ def tile_attention_pa_kernel(tc, emb, W1, W2, W3, out_0, out_1, out_2):
         def rotate(k, m, g, acc):
             half = g % 2
             if k == 0:
-                prod = prod0
-            elif FIRST_PAIR <= k < PAIRED:
+                return
+            if FIRST_PAIR <= k < PAIRED:
                 if k % 2 == 0:
                     pair["prod"] = prodp.tile([P, 2048], F32, name="prod2")
                 prod = pair["prod"][:, 1024 * (k % 2) : 1024 * (k % 2) + 1024]
             else:
-                prod = prodp.tile([P, 1024], F32, name="prod", tag="prod2")
-            if k:
-                multiply(prod, acc, half, 0, 4)
-            if FIRST_PAIR <= k < PAIRED:
-                if k % 2 == 1:
-                    both = pair["prod"].rearrange("p (j a n) -> p j a n", a=2, n=256)
-                    y2 = yp.tile([P, 1024], F32, name="y2")
-                    nc.gpsimd.tensor_tensor(out=y2.rearrange("p (j n) -> p j n", n=256), in0=both[:, :, 0], in1=both[:, :, 1], op=ALU.add)
-                    nc.sync.dma_start(
-                        out=outs[g // 2][P * (m - 1) : P * (m + 1), 512 * half : 512 * half + 512].rearrange(
-                            "(j p) n -> p j n", p=P),
-                        in_=y2.rearrange("p (j n) -> p j n", n=512))
+                pair["prod"] = prodp.tile([P, 1024], F32, name="prod", tag="prod2")
+                prod = pair["prod"]
+            multiply(prod, acc, half, 0, 4)
+
+        def add(k, m, g):
+            paired = FIRST_PAIR <= k < PAIRED
+            if paired and k % 2 == 0:
                 return
-            y = yp.tile([P, 512], F32, name="y", tag="y2")
-            both = prod.rearrange("p (j a n) -> p j a n", a=2, n=256)
+            n = 2 if paired else 1
+            half = g % 2
+            both = (pair["prod"] if k else prod0).rearrange("p (j a n) -> p j a n", a=2, n=256)
+            y = yp.tile([P, 512 * n], F32, name="y")
             eng = nc.vector if k in VADDS else nc.gpsimd
             eng.tensor_tensor(out=y.rearrange("p (j n) -> p j n", n=256), in0=both[:, :, 0], in1=both[:, :, 1], op=ALU.add)
-            nc.sync.dma_start(out=outs[g // 2][P * m : P * m + P, 512 * half : 512 * half + 512], in_=y)
+            nc.sync.dma_start(
+                out=outs[g // 2][P * (m + 1 - n) : P * (m + 1), 512 * half : 512 * half + 512].rearrange(
+                    "(j p) n -> p j n", p=P),
+                in_=y.rearrange("p (j n) -> p j n", n=512))
 
         vaccs = {}
 
@@ -268,46 +268,46 @@ def tile_attention_pa_kernel(tc, emb, W1, W2, W3, out_0, out_1, out_2):
         banks = [(m, g) for g in range(4) for m in range(8)]
         accs = {}
 
-        ctx.enter_context(tc.manual_schedule(engines={mybir.EngineType.PE, mybir.EngineType.Activation,
-                                                      mybir.EngineType.DVE, mybir.EngineType.Pool}))
-        table_turns_v(0)
-        table_turns_g(1)
-        table_phase(0)
-        tx(0)
-        cpx(0, "v")
-        sine(0)
-        fold_phase(0)
-        quant_x(0, 1)
-        tw(0, 0)
-        tw(0, 1)
-        cpw(0, 0, "s")
-        cosine(0)
-        copy_sine(0)
-        cpw(0, 1, "v")
-        quant_w0(0)
-        quant_w0(1)
-        tw(0, 2)
-        tw(0, 3)
-        cpw(0, 2, "s")
-        cpw(0, 3, "v")
-        copy_cosine(0)
-        tx(1)
-        cpx(1, "s")
-        acc0 = [accp.tile([P, 256], F32, name="acc") for f in range(2)]
-        accs[0] = acc0
-        project0(acc0[0], 0)
-        multiply(prod0, acc0[0], 0, 0, 2)
-        quant_w0(2)
-        quant_w0(3)
-        quant_x(1, 2)
-        tx(2)
-        tx(3)
-        cpx(2, "s")
-        cpx(3, "s")
-        project0(acc0[1], 1)
-        accs[1] = project(accp, 1, 0)
-        multiply(prod0, acc0[1], 0, 2, 4)
-        quant_x(2, 4)
+        with tc.manual_schedule(engines={mybir.EngineType.PE, mybir.EngineType.Activation,
+                                         mybir.EngineType.DVE, mybir.EngineType.Pool}):
+            table_turns_v(0)
+            table_turns_g(1)
+            table_phase(0)
+            tx(0)
+            cpx(0, "v")
+            sine(0, 1, 1.0)
+            fold_phase(0)
+            quant_x(0, 1)
+            tw(0, 0)
+            tw(0, 1)
+            cpw(0, 0, "s")
+            cosine(0, 0)
+            copy_sine(0)
+            cpw(0, 1, "v")
+            quant_w0(0)
+            quant_w0(1)
+            tw(0, 2)
+            tw(0, 3)
+            cpw(0, 2, "s")
+            cpw(0, 3, "v")
+            copy_cosine(0)
+            tx(1)
+            cpx(1, "s")
+            acc0 = [accp.tile([P, 256], F32, name="acc") for f in range(2)]
+            accs[0] = acc0
+            project0(acc0[0], 0)
+            multiply(prod0, acc0[0], 0, 0, 2)
+            quant_w0(2)
+            quant_w0(3)
+            quant_x(1, 2)
+            tx(2)
+            tx(3)
+            cpx(2, "s")
+            cpx(3, "s")
+            project0(acc0[1], 1)
+            accs[1] = project(accp, 1, 0)
+            multiply(prod0, acc0[1], 0, 2, 4)
+            quant_x(2, 4)
 
         for k in range(32):
             if k < 2:
@@ -327,12 +327,12 @@ def tile_attention_pa_kernel(tc, emb, W1, W2, W3, out_0, out_1, out_2):
                 table_phase(1)
             if k == 3:
                 quant_x(6, 8)
-                sine(1)
+            if k == 4:
+                sine(1, 1, 1.0)
+                sine(1, 2, -1.0)
                 fold_phase(1)
-                cosine(1)
-            if k == 6:
-                copy_sine(1)
-                copy_cosine(1)
+                cosine(1, 0)
+                cosine(1, 3)
             if k in WQ:
                 quant_w(WQ[k])
             if k + LOOK < 32:
@@ -340,3 +340,4 @@ def tile_attention_pa_kernel(tc, emb, W1, W2, W3, out_0, out_1, out_2):
             if k >= V0 and k - V0 < 16:
                 value_mm(k - V0)
                 value_out(k - V0)
+            add(k, banks[k][0], banks[k][1])

import math
from contextlib import ExitStack

import concourse.mybir as mybir
from concourse.masks import make_identity

FLOPS = 2 * 1024 * 1024 * 3072

WQ = {5: 1, 9: 4, 13: 2, 17: 5, 21: 3}
TW = {2: (1, (0, 1)), 3: (1, (2, 3)), 5: (4, (0, 1)), 6: (4, (2, 3)), 8: (2, (0, 1)), 9: (2, (2, 3)),
      12: (5, (0, 1)), 13: (5, (2, 3)), 16: (3, (0, 1)), 17: (3, (2, 3))}
V0 = 11
VADDS = (29, 31)
LOOK = 2
FIRST_PAIR = 2
PAIRED = 28

F32 = mybir.dt.float32
BF16 = mybir.dt.bfloat16
I32 = mybir.dt.int32
U32 = mybir.dt.uint32
U8 = mybir.dt.uint8
FP8X4 = mybir.dt.float8_e4m3fn_x4
ALU = mybir.AluOpType
ACT = mybir.ActivationFunctionType

P = 128


def tile_attention_pa_kernel(tc, emb, W1, W2, W3, out_0, out_1, out_2):
    nc = tc.nc
    x2d = emb.flatten_outer_dims()
    weights = [W1, W2, W3]
    outs = [o.rearrange("b h (a c) d -> (b h a) (c d)", c=8) for o in (out_0, out_1, out_2)]

    with ExitStack() as ctx:
        const = ctx.enter_context(tc.tile_pool(name="const", bufs=1))
        gwp = ctx.enter_context(tc.tile_pool(name="gwp", bufs=2))
        prodp = ctx.enter_context(tc.tile_pool(name="prodp", bufs=5))
        yp = ctx.enter_context(tc.tile_pool(name="yp", bufs=6))
        vp = ctx.enter_context(tc.tile_pool(name="vp", bufs=6))
        tps = ctx.enter_context(tc.psum_pool(name="tps", bufs=3))
        accp = ctx.enter_context(tc.psum_pool(name="accp", bufs=3))
        accvp = ctx.enter_context(tc.psum_pool(name="accvp", bufs=2))

        xs = const.tile([P, 8192], BF16, name="xs")
        ws = [const.tile([P, 4096], BF16, name="ws%d" % g) for g in range(6)]
        gw0 = [const.tile([P, 1024], BF16, name="gw0_%d" % j, align_bytes=64) for j in range(4)]
        gx = const.tile([P, 8192], BF16, name="gx", align_bytes=64)
        cx = const.tile([P, 2048], U32, name="cx", align_bytes=64)
        sx = const.tile([P, 2048], U8, name="sx", align_bytes=64)
        cw = [const.tile([P, 1024], U32, name="cw%d" % g, align_bytes=64) for g in range(6)]
        sw = [const.tile([P, 1024], U8, name="sw%d" % g, align_bytes=64) for g in range(6)]
        ident = const.tile([P, P], F32, name="ident")
        pos = const.tile([P, 8], F32, name="pos")
        post = const.tile([P, 8], F32, name="post")
        freq = const.tile([P, 64], F32, name="freq")
        half_pi = const.tile([P, 1], F32, name="half_pi")
        warm = const.tile([P, 1], F32, name="warm")
        turns = [const.tile([P, 256], F32, name="turns%d" % h) for h in range(2)]
        whole = [const.tile([P, 256], I32, name="whole%d" % h) for h in range(2)]
        phase = [const.tile([P, 256], F32, name="phase%d" % h) for h in range(2)]
        fold = [const.tile([P, 256], F32, name="fold%d" % h) for h in range(2)]
        tab = const.tile([P, 2048], F32, name="tab")

        xs_w = xs.bitcast(F32)
        gx_w = gx.bitcast(F32)

        def load_x(j0, j1):
            nc.sync.dma_start(
                out=xs[:, 1024 * j0 : 1024 * j1].rearrange("p (j k) -> p j k", k=1024),
                in_=x2d[P * j0 : P * j1, :].rearrange("(j p) k -> p j k", p=P),
            )

        def load_w(g, b0, b1):
            r0 = 512 * (g % 2)
            nc.sync.dma_start(
                out=ws[g][:, 2048 * b0 : 2048 * b1].rearrange("p (b j) -> p b j", j=2048),
                in_=weights[g // 2][r0 + 256 * b0 : r0 + 256 * b1, :].rearrange("(b p j) k -> p b (j k)", p=P, j=2),
            )

        load_x(0, 1)
        load_w(0, 0, 1)
        load_w(0, 1, 2)
        load_x(1, 2)
        load_x(2, 4)
        load_x(4, 6)
        load_x(6, 8)
        for g in (1, 4, 2, 5, 3):
            load_w(g, 0, 2)

        nc.gpsimd.memset(warm, 0.0)
        nc.gpsimd.tensor_scalar(out=half_pi, in0=warm, scalar1=1.0, scalar2=0.5 * math.pi, op0=ALU.mult, op1=ALU.add)
        nc.scalar.activation(out=warm, in_=warm, func=ACT.Sin)
        nc.gpsimd.iota(pos[0:64, :], pattern=[[1, 8]], base=0, channel_multiplier=8,
                       allow_small_or_imprecise_dtypes=True)
        nc.gpsimd.iota(pos[64:128, :], pattern=[[1, 8]], base=0, channel_multiplier=8,
                       allow_small_or_imprecise_dtypes=True)
        make_identity(nc, ident)

        ratio = 10000.0 ** (-1.0 / 64.0)
        nc.vector.memset(freq[:, 0:1], 1.0)
        for e in range(6):
            w = 2 ** e
            nc.vector.tensor_scalar_mul(out=freq[:, w : 2 * w], in0=freq[:, 0:w], scalar1=ratio ** w)
        nc.vector.tensor_scalar_mul(out=post, in0=pos, scalar1=1.0 / (2.0 * math.pi))

        tab_s = tab.rearrange("p (h b q r) -> p h q b r", h=2, b=2, q=4)
        tab_v = tab.rearrange("p (h c s r) -> p h c r s", h=2, c=4, s=2)

        def angle_args(h):
            return (post[:, 4 * h : 4 * h + 4].unsqueeze(2).to_broadcast([P, 4, 64]),
                    freq.unsqueeze(1).to_broadcast([P, 4, 64]))

        def table_turns_v(h):
            in0, in1 = angle_args(h)
            nc.vector.tensor_tensor(out=turns[h].rearrange("p (c i) -> p c i", c=4), in0=in0, in1=in1, op=ALU.mult)
            nc.vector.scalar_tensor_tensor(out=whole[h].rearrange("p (c i) -> p c i", c=4), in0=in0,
                                           scalar=1.0, in1=in1, op0=ALU.mult, op1=ALU.mult)

        def table_turns_g(h):
            in0, in1 = angle_args(h)
            nc.gpsimd.tensor_tensor(out=turns[h].rearrange("p (c i) -> p c i", c=4), in0=in0, in1=in1, op=ALU.mult)
            nc.gpsimd.tensor_scalar(out=whole[h], in0=turns[h], scalar1=1.0, scalar2=0.0, op0=ALU.mult, op1=ALU.add)

        def table_phase(h):
            nc.vector.tensor_tensor(out=phase[h], in0=turns[h], in1=whole[h], op=ALU.subtract)

        def by_block(t):
            return t.rearrange("p (b r) -> p b r", b=2)

        def sine(h, q, sign):
            nc.scalar.activation(out=tab_s[:, h, q], in_=by_block(phase[h]), func=ACT.Sin, scale=sign * 2.0 * math.pi)

        def fold_phase(h):
            nc.scalar.activation(out=fold[h], in_=phase[h], func=ACT.Abs)

        def cosine(h, q):
            nc.scalar.activation(out=tab_s[:, h, q], in_=by_block(fold[h]), func=ACT.Sin, scale=-2.0 * math.pi, bias=half_pi)

        def copy_sine(h):
            nc.vector.tensor_scalar_mul(out=tab_s[:, h, 2], in0=tab_s[:, h, 1], scalar1=-1.0)

        def copy_cosine(h):
            nc.vector.tensor_copy(out=tab_s[:, h, 3], in_=tab_s[:, h, 0])

        tbanks = {}

        def transpose_rows(key, src_w, col0):
            bank = tps.tile([P, 512], F32, name="tbank")
            for q in range(4):
                c0 = col0 + 256 * (q // 2)
                nc.tensor.transpose(out=bank[:, P * q : P * q + P], in_=src_w[:, c0 + q % 2 : c0 + 256 : 2], identity=ident)
            tbanks[key] = bank

        def regroup(eng, dst, key):
            src = tbanks[key].rearrange("p (g u r) -> p g r u", g=2, u=2)
            if eng == "s":
                nc.scalar.copy(out=dst, in_=src)
            else:
                nc.vector.tensor_copy(out=dst, in_=src)

        def tx(j):
            transpose_rows(("x", j), xs_w, 512 * j)

        def cpx(j, eng):
            regroup(eng, gx_w[:, 512 * j : 512 * j + 512].rearrange("p (g r u) -> p g r u", g=2, u=2), ("x", j))

        def quant_x(j0, j1):
            nc.vector.quantize_mx(out=cx[:, 256 * j0 : 256 * j1].bitcast(FP8X4),
                                  scales=sx[:, 256 * j0 : 256 * j1], in_=gx[:, 1024 * j0 : 1024 * j1])

        gws = {}

        def tw(g, j):
            transpose_rows((g, j), ws[g].bitcast(F32), 512 * j)

        def cpw(g, j, eng):
            if g == 0:
                regroup(eng, gw0[j].bitcast(F32).rearrange("p (g n u) -> p g n u", g=2, u=2), (g, j))
                return
            if g not in gws:
                gws[g] = gwp.tile([P, 4096], BF16, name="gw", align_bytes=64)
            dst4 = gws[g].bitcast(F32).rearrange("p (g n u) -> p g n u", g=2, u=2)
            regroup(eng, dst4[:, :, P * j : P * j + P, :], (g, j))

        def quant_w(g):
            nc.vector.quantize_mx(out=cw[g].bitcast(FP8X4), scales=sw[g], in_=gws[g])

        def quant_w0(j):
            for h in range(2):
                c0 = 512 * h + P * j
                nc.vector.quantize_mx(out=cw[0][:, c0 : c0 + P].bitcast(FP8X4), scales=sw[0][:, c0 : c0 + P],
                                      in_=gw0[j][:, 512 * h : 512 * h + 512])

        def project0(acc, f):
            for h in range(2):
                c0 = 512 * h + 256 * f
                nc.tensor.matmul_mx(out=acc,
                                    lhsT=cx[:, P * h : P * h + P].bitcast(FP8X4), lhsT_scale=sx[:, P * h : P * h + P],
                                    rhs=cw[0][:, c0 : c0 + 256].bitcast(FP8X4), rhs_scale=sw[0][:, c0 : c0 + 256],
                                    start=(h == 0), stop=(h == 1))

        def project(pool, m, g):
            acc = pool.tile([P, 512], F32, name="acc")
            for h in range(2):
                c0 = 256 * m + P * h
                nc.tensor.matmul_mx(out=acc,
                                    lhsT=cx[:, c0 : c0 + P].bitcast(FP8X4), lhsT_scale=sx[:, c0 : c0 + P],
                                    rhs=cw[g][:, 512 * h : 512 * h + 512].bitcast(FP8X4),
                                    rhs_scale=sw[g][:, 512 * h : 512 * h + 512],
                                    start=(h == 0), stop=(h == 1))
            return acc

        pair = {}

        def multiply(prod, acc, half, c0, c1):
            nc.vector.tensor_tensor(
                out=prod.rearrange("p (c r s) -> p c r s", c=4, s=2)[:, c0:c1],
                in0=acc.rearrange("p (c r) -> p c r", r=P).unsqueeze(3).to_broadcast([P, c1 - c0, P, 2]),
                in1=tab_v[:, half, c0:c1],
                op=ALU.mult,
            )

        prod0 = prodp.tile([P, 1024], F32, name="prod", tag="prod2")

        def rotate(k, m, g, acc):
            half = g % 2
            if k == 0:
                return
            if FIRST_PAIR <= k < PAIRED:
                if k % 2 == 0:
                    pair["prod"] = prodp.tile([P, 2048], F32, name="prod2")
                prod = pair["prod"][:, 1024 * (k % 2) : 1024 * (k % 2) + 1024]
            else:
                pair["prod"] = prodp.tile([P, 1024], F32, name="prod", tag="prod2")
                prod = pair["prod"]
            multiply(prod, acc, half, 0, 4)

        def add(k, m, g):
            paired = FIRST_PAIR <= k < PAIRED
            if paired and k % 2 == 0:
                return
            n = 2 if paired else 1
            half = g % 2
            both = (pair["prod"] if k else prod0).rearrange("p (j a n) -> p j a n", a=2, n=256)
            y = yp.tile([P, 512 * n], F32, name="y")
            eng = nc.vector if k in VADDS else nc.gpsimd
            eng.tensor_tensor(out=y.rearrange("p (j n) -> p j n", n=256), in0=both[:, :, 0], in1=both[:, :, 1], op=ALU.add)
            nc.sync.dma_start(
                out=outs[g // 2][P * (m + 1 - n) : P * (m + 1), 512 * half : 512 * half + 512].rearrange(
                    "(j p) n -> p j n", p=P),
                in_=y.rearrange("p (j n) -> p j n", n=512))

        vaccs = {}

        def value_mm(i):
            vaccs[i] = project(accvp, i % 8, 4 + i // 8)

        def value_out(i):
            m = i % 8
            half = i // 8
            v = vp.tile([P, 512], F32, name="v")
            nc.scalar.copy(out=v.rearrange("p (b r j) -> p b r j", b=2, j=2),
                           in_=vaccs[i].rearrange("p (b j r) -> p b r j", b=2, j=2))
            nc.sync.dma_start(out=outs[2][P * m : P * m + P, 512 * half : 512 * half + 512], in_=v)

        banks = [(m, g) for g in range(4) for m in range(8)]
        accs = {}

        with tc.manual_schedule(engines={mybir.EngineType.PE, mybir.EngineType.Activation,
                                         mybir.EngineType.DVE, mybir.EngineType.Pool}):
            table_turns_v(0)
            table_turns_g(1)
            table_phase(0)
            tx(0)
            cpx(0, "v")
            sine(0, 1, 1.0)
            fold_phase(0)
            quant_x(0, 1)
            tw(0, 0)
            tw(0, 1)
            cpw(0, 0, "s")
            cosine(0, 0)
            copy_sine(0)
            cpw(0, 1, "v")
            quant_w0(0)
            quant_w0(1)
            tw(0, 2)
            tw(0, 3)
            cpw(0, 2, "s")
            cpw(0, 3, "v")
            copy_cosine(0)
            tx(1)
            cpx(1, "s")
            acc0 = [accp.tile([P, 256], F32, name="acc") for f in range(2)]
            accs[0] = acc0
            project0(acc0[0], 0)
            multiply(prod0, acc0[0], 0, 0, 2)
            quant_w0(2)
            quant_w0(3)
            quant_x(1, 2)
            tx(2)
            tx(3)
            cpx(2, "s")
            cpx(3, "s")
            project0(acc0[1], 1)
            accs[1] = project(accp, 1, 0)
            multiply(prod0, acc0[1], 0, 2, 4)
            quant_x(2, 4)

        for k in range(32):
            if k < 2:
                for j in (4 + 2 * k, 5 + 2 * k):
                    tx(j)
                for j in (4 + 2 * k, 5 + 2 * k):
                    cpx(j, "s")
            if k in TW:
                g, js = TW[k]
                for j in js:
                    tw(g, j)
                for j in js:
                    cpw(g, j, "s")
            rotate(k, banks[k][0], banks[k][1], accs[k])
            if k == 2:
                quant_x(4, 6)
                table_phase(1)
            if k == 3:
                quant_x(6, 8)
            if k == 4:
                sine(1, 1, 1.0)
                sine(1, 2, -1.0)
                fold_phase(1)
                cosine(1, 0)
                cosine(1, 3)
            if k in WQ:
                quant_w(WQ[k])
            if k + LOOK < 32:
                accs[k + LOOK] = project(accp, banks[k + LOOK][0], banks[k + LOOK][1])
            if k >= V0 and k - V0 < 16:
                value_mm(k - V0)
                value_out(k - V0)
            add(k, banks[k][0], banks[k][1])
